import numpy as np
import ml_dtypes

BF16 = ml_dtypes.bfloat16


def bf(x):
    return np.asarray(x, np.float32).astype(BF16)


def f32(x):
    return np.asarray(x, np.float32)


def f64(x):
    return np.asarray(x).astype(np.float64)


def striped(idx):
    return np.tile(idx.reshape(-1, 16).T, (8, 1))


C, S, T, K, N = 512, 2048, 1024, 4, 4096
BIAS_SCALE = 0.1


def setup_inputs():
    return {"emb": f32(np.random.standard_normal((C, S))), "attn": f32(np.random.standard_normal((C, T))), "wout": bf(np.random.standard_normal((C, C)) / np.sqrt(C)), "bout": f32(0.1 * np.random.standard_normal((C, 1))), "offs": striped(np.random.permutation(np.tile(np.arange(S), 2))[:N])}


def reference(emb, attn, wout, bout, offs):
    idx = offs[:16].T.reshape(-1)
    h = f64(attn) + BIAS_SCALE * f64(emb)[:, idx].reshape(C, K, T).sum(axis=1)
    return f64(wout).T @ h + f64(bout)

@@ -1,0 +1,65 @@
+import concourse.mybir as mybir
+
+P = 128
+C, S, T, K = 512, 2048, 1024, 4
+BIAS_SCALE = 0.1
+CB = C // P
+TP = 512
+NP = T // TP
+FLOPS = 2 * C * C * T
+
+F32, BF16, U16 = mybir.dt.float32, mybir.dt.bfloat16, mybir.dt.uint16
+ADD = mybir.AluOpType.add
+IDENTITY = mybir.ActivationFunctionType.Identity
+
+
+def tile_baseattention_kernel(tc, emb, attn, wout, bout, offs, out):
+    nc = tc.nc
+    with (
+        tc.tile_pool(name="held", bufs=1) as held,
+        tc.tile_pool(name="work", bufs=4) as work,
+        tc.psum_pool(name="psum", bufs=2) as psum,
+    ):
+        offsets = held.tile([P, K * T // 16], U16, name="offsets")
+        nc.sync.dma_start(offsets[:], offs)
+        weights = held.tile([P, CB, C], BF16, name="weights")
+        table = [held.tile([P, S], F32, name=f"table{cb}") for cb in range(CB)]
+        attn_in = [[held.tile([P, TP], F32, name=f"attn{tp}_{cb}") for cb in range(CB)] for tp in range(NP)]
+        for tp in range(NP):
+            for cb in range(CB):
+                rows = slice(cb * P, (cb + 1) * P)
+                nc.sync.dma_start(attn_in[tp][cb][:], attn[rows, tp * TP : (tp + 1) * TP])
+                if tp == 0:
+                    nc.sync.dma_start(table[cb][:], emb[rows, :])
+                if tp == 0 and cb == 0:
+                    nc.sync.dma_start(weights[:], wout.rearrange("(cb p) m -> p cb m", p=P))
+        bias = held.tile([P, CB], F32, name="bias")
+        with nc.allow_non_contiguous_dma(reason="bout: one float32 for each partition and block"):
+            nc.sync.dma_start(bias[:], bout.rearrange("(mb p) one -> p (mb one)", p=P))
+
+        for tp in range(NP):
+            tokens = slice(tp * TP, (tp + 1) * TP)
+            proj = [psum.tile([P, TP], F32, name=f"proj{mb}") for mb in range(CB)]
+            for cb in range(CB):
+                total = work.tile([P, TP], F32, name="total")
+                nc.scalar.mul(total[:], attn_in[tp][cb][:], 1.0 / BIAS_SCALE)
+                for k in range(K):
+                    first = (k * T + tp * TP) // 16
+                    picked = table[cb][:].indirect(offsets[:, first : first + TP // 16])
+                    grown = work.tile([P, TP], F32, name="total")
+                    nc.vector.tensor_tensor(grown[:], picked, total[:], ADD)
+                    total = grown
+                h = work.tile([P, TP], BF16, name="h")
+                nc.scalar.mul(h[:], total[:], BIAS_SCALE)
+                for mb in range(CB):
+                    nc.tensor.matmul(
+                        proj[mb][:],
+                        weights[:, cb, mb * P : (mb + 1) * P],
+                        h[:],
+                        start=(cb == 0),
+                        stop=(cb == CB - 1),
+                    )
+            for mb in range(CB):
+                result = work.tile([P, TP], F32, name="result")
+                nc.scalar.activation(result[:], proj[mb][:], IDENTITY, bias=bias[:, mb : mb + 1])
+                nc.sync.dma_start(out[mb * P : (mb + 1) * P, tokens], result[:])

@@ -41,7 +41,7 @@ def tile_baseattention_kernel(tc, emb, attn, wout, bout, offs, out):
             tokens = slice(tp * TP, (tp + 1) * TP)
             proj = [psum.tile([P, TP], F32, name=f"proj{mb}") for mb in range(CB)]
             for cb in range(CB):
-                total = work.tile([P, TP], F32, name="total")
+                total = work.tile([P, TP], F32, name="seed")
                 nc.scalar.mul(total[:], attn_in[tp][cb][:], 1.0 / BIAS_SCALE)
                 for k in range(K):
                     first = (k * T + tp * TP) // 16

@@ -6,6 +6,7 @@ BIAS_SCALE = 0.1
 CB = C // P
 TP = 512
 NP = T // TP
+HALF = TP // 2
 FLOPS = 2 * C * C * T
 
 F32, BF16, U16 = mybir.dt.float32, mybir.dt.bfloat16, mybir.dt.uint16
@@ -41,16 +42,19 @@ def tile_baseattention_kernel(tc, emb, attn, wout, bout, offs, out):
             tokens = slice(tp * TP, (tp + 1) * TP)
             proj = [psum.tile([P, TP], F32, name=f"proj{mb}") for mb in range(CB)]
             for cb in range(CB):
-                total = work.tile([P, TP], F32, name="seed")
-                nc.scalar.mul(total[:], attn_in[tp][cb][:], 1.0 / BIAS_SCALE)
+                seed = work.tile([P, TP], F32, name="seed")
+                nc.scalar.mul(seed[:], attn_in[tp][cb][:], 1.0 / BIAS_SCALE)
+                total = [seed[:, half * HALF : (half + 1) * HALF] for half in range(2)]
                 for k in range(K):
-                    first = (k * T + tp * TP) // 16
-                    picked = table[cb][:].indirect(offsets[:, first : first + TP // 16])
-                    grown = work.tile([P, TP], F32, name="total")
-                    nc.vector.tensor_tensor(grown[:], picked, total[:], ADD)
-                    total = grown
+                    for half in range(2):
+                        first = (k * T + tp * TP + half * HALF) // 16
+                        picked = table[cb][:].indirect(offsets[:, first : first + HALF // 16])
+                        grown = work.tile([P, HALF], F32, name=f"total{half}")
+                        nc.vector.tensor_tensor(grown[:], picked, total[half], ADD)
+                        total[half] = grown[:]
                 h = work.tile([P, TP], BF16, name="h")
-                nc.scalar.mul(h[:], total[:], BIAS_SCALE)
+                for half in range(2):
+                    nc.scalar.mul(h[:, half * HALF : (half + 1) * HALF], total[half], BIAS_SCALE)
                 for mb in range(CB):
                     nc.tensor.matmul(
                         proj[mb][:],

@@ -19,7 +19,8 @@ def tile_baseattention_kernel(tc, emb, attn, wout, bout, offs, out):
     with (
         tc.tile_pool(name="held", bufs=1) as held,
         tc.tile_pool(name="work", bufs=4) as work,
-        tc.psum_pool(name="psum", bufs=2) as psum,
+        tc.tile_pool(name="leave", bufs=8) as leave,
+        tc.psum_pool(name="psum", bufs=1) as psum,
     ):
         offsets = held.tile([P, K * T // 16], U16, name="offsets")
         nc.sync.dma_start(offsets[:], offs)
@@ -39,8 +40,7 @@ def tile_baseattention_kernel(tc, emb, attn, wout, bout, offs, out):
             nc.sync.dma_start(bias[:], bout.rearrange("(mb p) one -> p (mb one)", p=P))
 
         for tp in range(NP):
-            tokens = slice(tp * TP, (tp + 1) * TP)
-            proj = [psum.tile([P, TP], F32, name=f"proj{mb}") for mb in range(CB)]
+            proj = [[psum.tile([P, HALF], F32, name=f"proj{half}_{mb}") for mb in range(CB)] for half in range(2)]
             for cb in range(CB):
                 seed = work.tile([P, TP], F32, name="seed")
                 nc.scalar.mul(seed[:], attn_in[tp][cb][:], 1.0 / BIAS_SCALE)
@@ -55,15 +55,20 @@ def tile_baseattention_kernel(tc, emb, attn, wout, bout, offs, out):
                 h = work.tile([P, TP], BF16, name="h")
                 for half in range(2):
                     nc.scalar.mul(h[:, half * HALF : (half + 1) * HALF], total[half], BIAS_SCALE)
+                    for mb in range(CB):
+                        nc.tensor.matmul(
+                            proj[half][mb][:],
+                            weights[:, cb, mb * P : (mb + 1) * P],
+                            h[:, half * HALF : (half + 1) * HALF],
+                            start=(cb == 0),
+                            stop=(cb == CB - 1),
+                        )
+            for half in range(2):
                 for mb in range(CB):
-                    nc.tensor.matmul(
-                        proj[mb][:],
-                        weights[:, cb, mb * P : (mb + 1) * P],
-                        h[:],
-                        start=(cb == 0),
-                        stop=(cb == CB - 1),
-                    )
-            for mb in range(CB):
-                result = work.tile([P, TP], F32, name="result")
-                nc.scalar.activation(result[:], proj[mb][:], IDENTITY, bias=bias[:, mb : mb + 1])
-                nc.sync.dma_start(out[mb * P : (mb + 1) * P, tokens], result[:])
+                    result = leave.tile([P, HALF], F32, name="result")
+                    if tp == NP - 1 and mb % 2 == 1:
+                        nc.vector.tensor_scalar_add(result[:], proj[half][mb][:], bias[:, mb : mb + 1])
+                    else:
+                        nc.scalar.activation(result[:], proj[half][mb][:], IDENTITY, bias=bias[:, mb : mb + 1])
+                    first_token = tp * TP + half * HALF
+                    nc.sync.dma_start(out[mb * P : (mb + 1) * P, first_token : first_token + HALF], result[:])

@@ -4,9 +4,9 @@ P = 128
 C, S, T, K = 512, 2048, 1024, 4
 BIAS_SCALE = 0.1
 CB = C // P
-TP = 512
-NP = T // TP
-HALF = TP // 2
+LAST = 128
+MAIN = T - LAST
+HALF = MAIN // 2
 FLOPS = 2 * C * C * T
 
 F32, BF16, U16 = mybir.dt.float32, mybir.dt.bfloat16, mybir.dt.uint16
@@ -26,49 +26,76 @@ def tile_baseattention_kernel(tc, emb, attn, wout, bout, offs, out):
         nc.sync.dma_start(offsets[:], offs)
         weights = held.tile([P, CB, C], BF16, name="weights")
         table = [held.tile([P, S], F32, name=f"table{cb}") for cb in range(CB)]
-        attn_in = [[held.tile([P, TP], F32, name=f"attn{tp}_{cb}") for cb in range(CB)] for tp in range(NP)]
-        for tp in range(NP):
-            for cb in range(CB):
-                rows = slice(cb * P, (cb + 1) * P)
-                nc.sync.dma_start(attn_in[tp][cb][:], attn[rows, tp * TP : (tp + 1) * TP])
-                if tp == 0:
-                    nc.sync.dma_start(table[cb][:], emb[rows, :])
-                if tp == 0 and cb == 0:
-                    nc.sync.dma_start(weights[:], wout.rearrange("(cb p) m -> p cb m", p=P))
+        attn_main = [held.tile([P, MAIN], F32, name=f"attn_main{cb}") for cb in range(CB)]
+        for cb in range(CB):
+            rows = slice(cb * P, (cb + 1) * P)
+            nc.sync.dma_start(attn_main[cb][:], attn[rows, 0:MAIN])
+            nc.sync.dma_start(table[cb][:], emb[rows, :])
+            if cb == 0:
+                nc.sync.dma_start(weights[:], wout.rearrange("(cb p) m -> p cb m", p=P))
+        attn_last = held.tile([P, CB, LAST], F32, name="attn_last")
+        nc.sync.dma_start(attn_last[:], attn[:, MAIN:T].rearrange("(cb p) t -> p cb t", p=P))
         bias = held.tile([P, CB], F32, name="bias")
         with nc.allow_non_contiguous_dma(reason="bout: one float32 for each partition and block"):
             nc.sync.dma_start(bias[:], bout.rearrange("(mb p) one -> p (mb one)", p=P))
 
-        for tp in range(NP):
-            proj = [[psum.tile([P, HALF], F32, name=f"proj{half}_{mb}") for mb in range(CB)] for half in range(2)]
-            for cb in range(CB):
-                seed = work.tile([P, TP], F32, name="seed")
-                nc.scalar.mul(seed[:], attn_in[tp][cb][:], 1.0 / BIAS_SCALE)
-                total = [seed[:, half * HALF : (half + 1) * HALF] for half in range(2)]
-                for k in range(K):
-                    for half in range(2):
-                        first = (k * T + tp * TP + half * HALF) // 16
-                        picked = table[cb][:].indirect(offsets[:, first : first + HALF // 16])
-                        grown = work.tile([P, HALF], F32, name=f"total{half}")
-                        nc.vector.tensor_tensor(grown[:], picked, total[half], ADD)
-                        total[half] = grown[:]
-                h = work.tile([P, TP], BF16, name="h")
+        def add_template(cb, k, first_token, tokens, total, lane):
+            first = (k * T + first_token) // 16
+            picked = table[cb][:].indirect(offsets[:, first : first + tokens // 16])
+            grown = work.tile([P, tokens], F32, name=f"total{lane}")
+            nc.vector.tensor_tensor(grown[:], picked, total, ADD)
+            return grown[:]
+
+
+        proj = [[psum.tile([P, HALF], F32, name=f"proj{half}_{mb}") for mb in range(CB)] for half in range(2)]
+        for cb in range(CB):
+            seed = work.tile([P, MAIN], F32, name="seed")
+            nc.scalar.mul(seed[:], attn_main[cb][:], 1.0 / BIAS_SCALE)
+            total = [seed[:, half * HALF : (half + 1) * HALF] for half in range(2)]
+            for k in range(K):
                 for half in range(2):
-                    nc.scalar.mul(h[:, half * HALF : (half + 1) * HALF], total[half], BIAS_SCALE)
-                    for mb in range(CB):
-                        nc.tensor.matmul(
-                            proj[half][mb][:],
-                            weights[:, cb, mb * P : (mb + 1) * P],
-                            h[:, half * HALF : (half + 1) * HALF],
-                            start=(cb == 0),
-                            stop=(cb == CB - 1),
-                        )
+                    total[half] = add_template(cb, k, half * HALF, HALF, total[half], half)
+            h = work.tile([P, MAIN], BF16, name="h")
             for half in range(2):
+                nc.scalar.mul(h[:, half * HALF : (half + 1) * HALF], total[half], BIAS_SCALE)
                 for mb in range(CB):
-                    result = leave.tile([P, HALF], F32, name="result")
-                    if tp == NP - 1 and mb % 2 == 1:
-                        nc.vector.tensor_scalar_add(result[:], proj[half][mb][:], bias[:, mb : mb + 1])
-                    else:
-                        nc.scalar.activation(result[:], proj[half][mb][:], IDENTITY, bias=bias[:, mb : mb + 1])
-                    first_token = tp * TP + half * HALF
-                    nc.sync.dma_start(out[mb * P : (mb + 1) * P, first_token : first_token + HALF], result[:])
+                    nc.tensor.matmul(
+                        proj[half][mb][:],
+                        weights[:, cb, mb * P : (mb + 1) * P],
+                        h[:, half * HALF : (half + 1) * HALF],
+                        start=(cb == 0),
+                        stop=(cb == CB - 1),
+                    )
+        seed_last = held.tile([P, CB, LAST], F32, name="seed_last")
+        nc.scalar.mul(seed_last[:], attn_last[:], 1.0 / BIAS_SCALE)
+        for half in range(2):
+            for mb in range(CB):
+                result = leave.tile([P, HALF], F32, name="result")
+                nc.scalar.activation(result[:], proj[half][mb][:], IDENTITY, bias=bias[:, mb : mb + 1])
+                nc.sync.dma_start(out[mb * P : (mb + 1) * P, half * HALF : (half + 1) * HALF], result[:])
+
+        proj_last = [psum.tile([P, LAST], F32, name=f"proj0_{mb}") for mb in range(CB)]
+        h_last = held.tile([P, CB, LAST], BF16, name="h_last")
+        for pair in range(0, CB, 2):
+            total = [seed_last[:, pair + lane, :] for lane in range(2)]
+            for k in range(K):
+                for lane in range(2):
+                    total[lane] = add_template(pair + lane, k, MAIN, LAST, total[lane], lane)
+            for lane in range(2):
+                cb = pair + lane
+                nc.scalar.mul(h_last[:, cb, :], total[lane], BIAS_SCALE)
+                for mb in range(CB):
+                    nc.tensor.matmul(
+                        proj_last[mb][:],
+                        weights[:, cb, mb * P : (mb + 1) * P],
+                        h_last[:, cb, :],
+                        start=(cb == 0),
+                        stop=(cb == CB - 1),
+                    )
+        for mb in range(CB):
+            result = leave.tile([P, LAST], F32, name="result")
+            if mb % 2 == 1:
+                nc.vector.tensor_scalar_add(result[:], proj_last[mb][:], bias[:, mb : mb + 1])
+            else:
+                nc.scalar.activation(result[:], proj_last[mb][:], IDENTITY, bias=bias[:, mb : mb + 1])
+            nc.sync.dma_start(out[mb * P : (mb + 1) * P, MAIN:T], result[:])

@@ -98,4 +98,5 @@ def tile_baseattention_kernel(tc, emb, attn, wout, bout, offs, out):
                 nc.vector.tensor_scalar_add(result[:], proj_last[mb][:], bias[:, mb : mb + 1])
             else:
                 nc.scalar.activation(result[:], proj_last[mb][:], IDENTITY, bias=bias[:, mb : mb + 1])
-            nc.sync.dma_start(out[mb * P : (mb + 1) * P, MAIN:T], result[:])
+            queue = nc.sync if mb % 2 == 1 else nc.scalar
+            queue.dma_start(out[mb * P : (mb + 1) * P, MAIN:T], result[:])

@@ -6,7 +6,7 @@ BIAS_SCALE = 0.1
 CB = C // P
 LAST = 128
 MAIN = T - LAST
-HALF = MAIN // 2
+PARTS = [(0, 512), (512, MAIN - 512)]
 FLOPS = 2 * C * C * T
 
 F32, BF16, U16 = mybir.dt.float32, mybir.dt.bfloat16, mybir.dt.uint16
@@ -26,12 +26,17 @@ def tile_baseattention_kernel(tc, emb, attn, wout, bout, offs, out):
         nc.sync.dma_start(offsets[:], offs)
         weights = held.tile([P, CB, C], BF16, name="weights")
         table = [held.tile([P, S], F32, name=f"table{cb}") for cb in range(CB)]
-        attn_main = [held.tile([P, MAIN], F32, name=f"attn_main{cb}") for cb in range(CB)]
+        attn_main = [held.tile([P, MAIN], F32, name=f"attn_main{cb}") for cb in range(1, CB)]
+        attn_first = [held.tile([P, tokens], F32, name=f"attn_first{part}") for part, (start, tokens) in enumerate(PARTS)]
         for cb in range(CB):
             rows = slice(cb * P, (cb + 1) * P)
-            nc.sync.dma_start(attn_main[cb][:], attn[rows, 0:MAIN])
+            if cb == 0:
+                nc.sync.dma_start(attn_first[0][:], attn[rows, 0 : PARTS[1][0]])
+            else:
+                nc.sync.dma_start(attn_main[cb - 1][:], attn[rows, 0:MAIN])
             nc.sync.dma_start(table[cb][:], emb[rows, :])
             if cb == 0:
+                nc.sync.dma_start(attn_first[1][:], attn[rows, PARTS[1][0] : MAIN])
                 nc.sync.dma_start(weights[:], wout.rearrange("(cb p) m -> p cb m", p=P))
         attn_last = held.tile([P, CB, LAST], F32, name="attn_last")
         nc.sync.dma_start(attn_last[:], attn[:, MAIN:T].rearrange("(cb p) t -> p cb t", p=P))
@@ -42,37 +47,44 @@ def tile_baseattention_kernel(tc, emb, attn, wout, bout, offs, out):
         def add_template(cb, k, first_token, tokens, total, lane):
             first = (k * T + first_token) // 16
             picked = table[cb][:].indirect(offsets[:, first : first + tokens // 16])
-            grown = work.tile([P, tokens], F32, name=f"total{lane}")
+            if (cb, k, first_token) == (0, 1, 0):
+                grown = held.tile([P, tokens], F32, name="grown_late", tag="attn_first1")
+            else:
+                grown = work.tile([P, tokens], F32, name=f"total{lane}")
             nc.vector.tensor_tensor(grown[:], picked, total, ADD)
             return grown[:]
 
 
-        proj = [[psum.tile([P, HALF], F32, name=f"proj{half}_{mb}") for mb in range(CB)] for half in range(2)]
+        proj = [[psum.tile([P, tokens], F32, name=f"proj{half}_{mb}") for mb in range(CB)] for half, (start, tokens) in enumerate(PARTS)]
         for cb in range(CB):
             seed = work.tile([P, MAIN], F32, name="seed")
-            nc.scalar.mul(seed[:], attn_main[cb][:], 1.0 / BIAS_SCALE)
-            total = [seed[:, half * HALF : (half + 1) * HALF] for half in range(2)]
+            if cb == 0:
+                for part, (start, tokens) in enumerate(PARTS):
+                    nc.scalar.mul(seed[:, start : start + tokens], attn_first[part][:], 1.0 / BIAS_SCALE)
+            else:
+                nc.scalar.mul(seed[:], attn_main[cb - 1][:], 1.0 / BIAS_SCALE)
+            total = [seed[:, start : start + tokens] for start, tokens in PARTS]
             for k in range(K):
-                for half in range(2):
-                    total[half] = add_template(cb, k, half * HALF, HALF, total[half], half)
+                for half, (start, tokens) in enumerate(PARTS):
+                    total[half] = add_template(cb, k, start, tokens, total[half], half)
             h = work.tile([P, MAIN], BF16, name="h")
-            for half in range(2):
-                nc.scalar.mul(h[:, half * HALF : (half + 1) * HALF], total[half], BIAS_SCALE)
+            for half, (start, tokens) in enumerate(PARTS):
+                nc.scalar.mul(h[:, start : start + tokens], total[half], BIAS_SCALE)
                 for mb in range(CB):
                     nc.tensor.matmul(
                         proj[half][mb][:],
                         weights[:, cb, mb * P : (mb + 1) * P],
-                        h[:, half * HALF : (half + 1) * HALF],
+                        h[:, start : start + tokens],
                         start=(cb == 0),
                         stop=(cb == CB - 1),
                     )
         seed_last = held.tile([P, CB, LAST], F32, name="seed_last")
         nc.scalar.mul(seed_last[:], attn_last[:], 1.0 / BIAS_SCALE)
-        for half in range(2):
+        for half, (start, tokens) in enumerate(PARTS):
             for mb in range(CB):
-                result = leave.tile([P, HALF], F32, name="result")
+                result = leave.tile([P, tokens], F32, name="result")
                 nc.scalar.activation(result[:], proj[half][mb][:], IDENTITY, bias=bias[:, mb : mb + 1])
-                nc.sync.dma_start(out[mb * P : (mb + 1) * P, half * HALF : (half + 1) * HALF], result[:])
+                nc.sync.dma_start(out[mb * P : (mb + 1) * P, start : start + tokens], result[:])
 
         proj_last = [psum.tile([P, LAST], F32, name=f"proj0_{mb}") for mb in range(CB)]
         h_last = held.tile([P, CB, LAST], BF16, name="h_last")

@@ -32,9 +32,11 @@ def tile_baseattention_kernel(tc, emb, attn, wout, bout, offs, out):
             rows = slice(cb * P, (cb + 1) * P)
             if cb == 0:
                 nc.sync.dma_start(attn_first[0][:], attn[rows, 0 : PARTS[1][0]])
-            else:
+            elif cb != 2:
                 nc.sync.dma_start(attn_main[cb - 1][:], attn[rows, 0:MAIN])
             nc.sync.dma_start(table[cb][:], emb[rows, :])
+            if cb == 2:
+                nc.sync.dma_start(attn_main[cb - 1][:], attn[rows, 0:MAIN])
             if cb == 0:
                 nc.sync.dma_start(attn_first[1][:], attn[rows, PARTS[1][0] : MAIN])
                 nc.sync.dma_start(weights[:], wout.rearrange("(cb p) m -> p cb m", p=P))
@@ -44,40 +46,56 @@ def tile_baseattention_kernel(tc, emb, attn, wout, bout, offs, out):
         with nc.allow_non_contiguous_dma(reason="bout: one float32 for each partition and block"):
             nc.sync.dma_start(bias[:], bout.rearrange("(mb p) one -> p (mb one)", p=P))
 
+        late_rows = {0: "attn_first1", 1: "attn_main2"}
+
         def add_template(cb, k, first_token, tokens, total, lane):
             first = (k * T + first_token) // 16
             picked = table[cb][:].indirect(offsets[:, first : first + tokens // 16])
-            if (cb, k, first_token) == (0, 1, 0):
-                grown = held.tile([P, tokens], F32, name="grown_late", tag="attn_first1")
+            if k == 1 and lane == 0 and cb in late_rows:
+                grown = held.tile([P, tokens], F32, name=f"late{cb}", tag=late_rows[cb])
             else:
                 grown = work.tile([P, tokens], F32, name=f"total{lane}")
             nc.vector.tensor_tensor(grown[:], picked, total, ADD)
             return grown[:]
 
 
-        proj = [[psum.tile([P, tokens], F32, name=f"proj{half}_{mb}") for mb in range(CB)] for half, (start, tokens) in enumerate(PARTS)]
-        for cb in range(CB):
+        proj = [
+            [psum.tile([P, tokens], F32, name=f"proj{part}_{mb}") for mb in range(CB)]
+            for part, (start, tokens) in enumerate(PARTS)
+        ]
+
+        def seed_main(cb):
             seed = work.tile([P, MAIN], F32, name="seed")
             if cb == 0:
                 for part, (start, tokens) in enumerate(PARTS):
                     nc.scalar.mul(seed[:, start : start + tokens], attn_first[part][:], 1.0 / BIAS_SCALE)
             else:
                 nc.scalar.mul(seed[:], attn_main[cb - 1][:], 1.0 / BIAS_SCALE)
-            total = [seed[:, start : start + tokens] for start, tokens in PARTS]
-            for k in range(K):
-                for half, (start, tokens) in enumerate(PARTS):
-                    total[half] = add_template(cb, k, start, tokens, total[half], half)
+            return seed
+
+        def round_and_project(cb, totals):
             h = work.tile([P, MAIN], BF16, name="h")
-            for half, (start, tokens) in enumerate(PARTS):
-                nc.scalar.mul(h[:, start : start + tokens], total[half], BIAS_SCALE)
+            for start, tokens, total in totals:
+                nc.scalar.mul(h[:, start : start + tokens], total, BIAS_SCALE)
+            for part, (start, tokens) in enumerate(PARTS):
                 for mb in range(CB):
                     nc.tensor.matmul(
-                        proj[half][mb][:],
+                        proj[part][mb][:],
                         weights[:, cb, mb * P : (mb + 1) * P],
                         h[:, start : start + tokens],
                         start=(cb == 0),
                         stop=(cb == CB - 1),
                     )
+
+        for blocks in ([0], [1, 2], [3]):
+            spans = [(cb, *part) for cb in blocks for part in (PARTS if len(blocks) == 1 else [(0, MAIN)])]
+            seeds = {cb: seed_main(cb) for cb in blocks}
+            total = [seeds[cb][:, start : start + tokens] for cb, start, tokens in spans]
+            for k in range(K):
+                for lane, (cb, start, tokens) in enumerate(spans):
+                    total[lane] = add_template(cb, k, start, tokens, total[lane], lane)
+            for cb in blocks:
+                round_and_project(cb, [(start, tokens, total[lane]) for lane, (block, start, tokens) in enumerate(spans) if block == cb])
         seed_last = held.tile([P, CB, LAST], F32, name="seed_last")
         nc.scalar.mul(seed_last[:], attn_last[:], 1.0 / BIAS_SCALE)
         for half, (start, tokens) in enumerate(PARTS):

import concourse.mybir as mybir

P = 128
C, S, T, K = 512, 2048, 1024, 4
BIAS_SCALE = 0.1
CB = C // P
LAST = 128
MAIN = T - LAST
PARTS = [(0, 512), (512, MAIN - 512)]
FLOPS = 2 * C * C * T

F32, BF16, U16 = mybir.dt.float32, mybir.dt.bfloat16, mybir.dt.uint16
ADD = mybir.AluOpType.add
IDENTITY = mybir.ActivationFunctionType.Identity


def tile_baseattention_kernel(tc, emb, attn, wout, bout, offs, out):
    nc = tc.nc
    with (
        tc.tile_pool(name="held", bufs=1) as held,
        tc.tile_pool(name="work", bufs=4) as work,
        tc.tile_pool(name="leave", bufs=8) as leave,
        tc.psum_pool(name="psum", bufs=1) as psum,
    ):
        offsets = held.tile([P, K * T // 16], U16, name="offsets")
        nc.sync.dma_start(offsets[:], offs)
        weights = held.tile([P, CB, C], BF16, name="weights")
        table = [held.tile([P, S], F32, name=f"table{cb}") for cb in range(CB)]
        attn_main = [held.tile([P, MAIN], F32, name=f"attn_main{cb}") for cb in range(1, CB)]
        attn_first = [held.tile([P, tokens], F32, name=f"attn_first{part}") for part, (start, tokens) in enumerate(PARTS)]
        for cb in range(CB):
            rows = slice(cb * P, (cb + 1) * P)
            if cb == 0:
                nc.sync.dma_start(attn_first[0][:], attn[rows, 0 : PARTS[1][0]])
            elif cb != 2:
                nc.sync.dma_start(attn_main[cb - 1][:], attn[rows, 0:MAIN])
            nc.sync.dma_start(table[cb][:], emb[rows, :])
            if cb == 2:
                nc.sync.dma_start(attn_main[cb - 1][:], attn[rows, 0:MAIN])
            if cb == 0:
                nc.sync.dma_start(attn_first[1][:], attn[rows, PARTS[1][0] : MAIN])
                nc.sync.dma_start(weights[:], wout.rearrange("(cb p) m -> p cb m", p=P))
        attn_last = held.tile([P, CB, LAST], F32, name="attn_last")
        nc.sync.dma_start(attn_last[:], attn[:, MAIN:T].rearrange("(cb p) t -> p cb t", p=P))
        bias = held.tile([P, CB], F32, name="bias")
        with nc.allow_non_contiguous_dma(reason="bout: one float32 for each partition and block"):
            nc.sync.dma_start(bias[:], bout.rearrange("(mb p) one -> p (mb one)", p=P))

        late_rows = {0: "attn_first1", 1: "attn_main2"}

        def add_template(cb, k, first_token, tokens, total, lane):
            first = (k * T + first_token) // 16
            picked = table[cb][:].indirect(offsets[:, first : first + tokens // 16])
            if k == 1 and lane == 0 and cb in late_rows:
                grown = held.tile([P, tokens], F32, name=f"late{cb}", tag=late_rows[cb])
            else:
                grown = work.tile([P, tokens], F32, name=f"total{lane}")
            nc.vector.tensor_tensor(grown[:], picked, total, ADD)
            return grown[:]


        proj = [
            [psum.tile([P, tokens], F32, name=f"proj{part}_{mb}") for mb in range(CB)]
            for part, (start, tokens) in enumerate(PARTS)
        ]

        def seed_main(cb):
            seed = work.tile([P, MAIN], F32, name="seed")
            if cb == 0:
                for part, (start, tokens) in enumerate(PARTS):
                    nc.scalar.mul(seed[:, start : start + tokens], attn_first[part][:], 1.0 / BIAS_SCALE)
            else:
                nc.scalar.mul(seed[:], attn_main[cb - 1][:], 1.0 / BIAS_SCALE)
            return seed

        def round_and_project(cb, totals):
            h = work.tile([P, MAIN], BF16, name="h")
            for start, tokens, total in totals:
                nc.scalar.mul(h[:, start : start + tokens], total, BIAS_SCALE)
            for part, (start, tokens) in enumerate(PARTS):
                for mb in range(CB):
                    nc.tensor.matmul(
                        proj[part][mb][:],
                        weights[:, cb, mb * P : (mb + 1) * P],
                        h[:, start : start + tokens],
                        start=(cb == 0),
                        stop=(cb == CB - 1),
                    )

        for blocks in ([0], [1, 2], [3]):
            spans = [(cb, *part) for cb in blocks for part in (PARTS if len(blocks) == 1 else [(0, MAIN)])]
            seeds = {cb: seed_main(cb) for cb in blocks}
            total = [seeds[cb][:, start : start + tokens] for cb, start, tokens in spans]
            for k in range(K):
                for lane, (cb, start, tokens) in enumerate(spans):
                    total[lane] = add_template(cb, k, start, tokens, total[lane], lane)
            for cb in blocks:
                round_and_project(cb, [(start, tokens, total[lane]) for lane, (block, start, tokens) in enumerate(spans) if block == cb])
        seed_last = held.tile([P, CB, LAST], F32, name="seed_last")
        nc.scalar.mul(seed_last[:], attn_last[:], 1.0 / BIAS_SCALE)
        for half, (start, tokens) in enumerate(PARTS):
            for mb in range(CB):
                result = leave.tile([P, tokens], F32, name="result")
                nc.scalar.activation(result[:], proj[half][mb][:], IDENTITY, bias=bias[:, mb : mb + 1])
                nc.sync.dma_start(out[mb * P : (mb + 1) * P, start : start + tokens], result[:])

        proj_last = [psum.tile([P, LAST], F32, name=f"proj0_{mb}") for mb in range(CB)]
        h_last = held.tile([P, CB, LAST], BF16, name="h_last")
        for pair in range(0, CB, 2):
            total = [seed_last[:, pair + lane, :] for lane in range(2)]
            for k in range(K):
                for lane in range(2):
                    total[lane] = add_template(pair + lane, k, MAIN, LAST, total[lane], lane)
            for lane in range(2):
                cb = pair + lane
                nc.scalar.mul(h_last[:, cb, :], total[lane], BIAS_SCALE)
                for mb in range(CB):
                    nc.tensor.matmul(
                        proj_last[mb][:],
                        weights[:, cb, mb * P : (mb + 1) * P],
                        h_last[:, cb, :],
                        start=(cb == 0),
                        stop=(cb == CB - 1),
                    )
        for mb in range(CB):
            result = leave.tile([P, LAST], F32, name="result")
            if mb % 2 == 1:
                nc.vector.tensor_scalar_add(result[:], proj_last[mb][:], bias[:, mb : mb + 1])
            else:
                nc.scalar.activation(result[:], proj_last[mb][:], IDENTITY, bias=bias[:, mb : mb + 1])
            queue = nc.sync if mb % 2 == 1 else nc.scalar
            queue.dma_start(out[mb * P : (mb + 1) * P, MAIN:T], result[:])
